import numpy as np
import ml_dtypes


def mxq(x, axis, fmt="e4m3"):
    dtype, down = {"e4m3": (ml_dtypes.float8_e4m3fn, 7), "e5m2": (ml_dtypes.float8_e5m2, 14)}[fmt]
    v = np.moveaxis(np.asarray(x, np.float32).astype(ml_dtypes.bfloat16).astype(np.float64), axis, -1)
    blocks = v.reshape(v.shape[:-1] + (-1, 32))
    amax = np.abs(blocks).max(-1, keepdims=True)
    byte = np.maximum(np.where(amax > 0, np.frexp(amax)[1] - 1 + 127, 0) - down, 1)
    scale = np.exp2(byte - 127.0)
    codes = (blocks / scale).astype(np.float32).astype(dtype).astype(np.float64)
    return np.moveaxis((codes * scale).reshape(v.shape), -1, axis)


WIDE = False


def mx_kscale(k):
    if not WIDE:
        return np.ones(k)
    levels = np.array([10, -10, 5, -5, 0])
    a = np.random.permutation(np.resize(levels, k // 512 * 4)).reshape(k // 512, 4)
    idx = np.arange(k)
    return np.exp2(a[idx // 512, idx % 128 // 32])


BF16 = ml_dtypes.bfloat16


def bf(x):
    return np.asarray(x, np.float32).astype(BF16)


def f64(x):
    return np.asarray(x).astype(np.float64)


B, S, HID, NH, HD, RD, RATIO = 4, 4096, 512, 2, 64, 32, 4
THETA = 10000.0
HALF = RD // 2


def rope_tables(positions):
    inv_freq = 1.0 / THETA ** (np.arange(HALF) / HALF)
    ang = positions[:, None] * inv_freq[None, :]
    return np.cos(ang), np.sin(ang)


def rope_interleaved(x, cos, sin):
    nope, rope = x[..., :-RD], x[..., -RD:]
    pr = rope.reshape(rope.shape[:-1] + (HALF, 2))
    a, b = pr[..., 0], pr[..., 1]
    new = np.stack([a * cos - b * sin, a * sin + b * cos], axis=-1).reshape(rope.shape)
    return np.concatenate([nope, new], axis=-1)


def setup_inputs():
    s = mx_kscale(HID)
    return {"hidden": bf(np.random.standard_normal((B, S, HID)) * s),
            "wq": bf(np.random.standard_normal((HID, NH * HD)) / np.sqrt(HID) / s[:, None])}


def reference(hidden, wq):
    q = mxq(f64(hidden), 2, "e4m3") @ mxq(f64(wq), 0, "e4m3")
    q = q.reshape(B, S, NH, HD).transpose(0, 2, 1, 3)
    cq, sq = rope_tables(np.arange(S))
    return rope_interleaved(q, cq, sq)

@@ -1,0 +1,289 @@
+import math
+from contextlib import ExitStack
+
+import concourse.mybir as mybir
+from concourse.masks import make_identity
+
+F32 = mybir.dt.float32
+BF16 = mybir.dt.bfloat16
+I32 = mybir.dt.int32
+U32 = mybir.dt.uint32
+U8 = mybir.dt.uint8
+FP8X4 = mybir.dt.float8_e4m3fn_x4
+ALU = mybir.AluOpType
+ACT = mybir.ActivationFunctionType
+
+P = 128
+BATCH, SEQ, HID = 4, 4096, 512
+HEADS, HEAD_DIM, ROPE_DIM = 2, 64, 32
+NOPE_DIM = HEAD_DIM - ROPE_DIM
+PAIRS = ROPE_DIM // 2
+FEATURES = HEADS * HEAD_DIM
+THETA = 10000.0
+FLOPS = 2 * BATCH * SEQ * HID * FEATURES
+
+WORDS = HID // 2
+TILES = SEQ // P
+GROUP = 4
+LOAD_TILES = 4
+STORE_TILES = 8
+N_GROUPS = BATCH * TILES // GROUP
+N_LOADS = BATCH * TILES // LOAD_TILES
+GROUPS_PER_LOAD = LOAD_TILES // GROUP
+GROUPS_PER_STORE = STORE_TILES // GROUP
+GROUPS_PER_BATCH = TILES // GROUP
+ROTATED = GROUP * HEADS * PAIRS
+
+ROUND = 1.5 * 2.0**23
+COARSE = 2.0**14
+
+
+def tile_deepseekv4attention_pb_t_kernel(tc, hidden, wq, out):
+    nc = tc.nc
+    with ExitStack() as ctx:
+        const = ctx.enter_context(tc.tile_pool(name="const", bufs=1))
+        xpool = ctx.enter_context(tc.tile_pool(name="xpool", bufs=N_LOADS))
+        gpool = ctx.enter_context(tc.tile_pool(name="gpool", bufs=3))
+        qpool = ctx.enter_context(tc.tile_pool(name="qpool", bufs=3))
+        rpool = ctx.enter_context(tc.tile_pool(name="rpool", bufs=2))
+        spool = ctx.enter_context(tc.tile_pool(name="spool", bufs=6))
+        tpsum = ctx.enter_context(tc.psum_pool(name="tpsum", bufs=4))
+        ypsum = ctx.enter_context(tc.psum_pool(name="ypsum", bufs=4))
+        ctx.enter_context(tc.manual_schedule())
+
+        w_raw = const.tile([P, 4, FEATURES], BF16)
+        for u in range(2):
+            nc.scalar.dma_start(
+                out=w_raw[:, 2 * u : 2 * u + 2, :],
+                in_=wq[WORDS * u : WORDS * (u + 1), :].rearrange("(q e) n -> q e n", e=2),
+            )
+        x_of = {}
+        for load in range(N_LOADS):
+            b, first = divmod(load * LOAD_TILES, TILES)
+            x_sb = xpool.tile([P, LOAD_TILES * HID], BF16)
+            nc.sync.dma_start(
+                out=x_sb[:],
+                in_=hidden[b].rearrange("(p c) k -> p (c k)", c=TILES)[
+                    :, first * HID : (first + LOAD_TILES) * HID
+                ],
+            )
+            x_of[load] = x_sb
+
+        position_i = const.tile([P, TILES], I32)
+        nc.gpsimd.iota(position_i[:], pattern=[[1, TILES]], base=0, channel_multiplier=TILES)
+        ident = const.tile([P, P], F32)
+        make_identity(nc, ident[:])
+
+        zero = const.tile([P, 1], F32)
+        nc.vector.memset(zero[:], 0.0)
+        warm = const.tile([P, 1], F32)
+        nc.scalar.activation(out=warm[:], in_=zero[:], func=ACT.Sin)
+
+        position = const.tile([P, TILES], F32)
+        nc.vector.tensor_copy(out=position[:], in_=position_i[:])
+        coarse = const.tile([P, TILES, PAIRS], F32)
+        fine = const.tile([P, TILES, PAIRS], F32)
+        for j in range(PAIRS):
+            turns = THETA ** (-j / PAIRS) / (2.0 * math.pi)
+            turns_coarse = round(turns * COARSE) / COARSE
+            nc.vector.tensor_scalar(
+                out=coarse[:, :, j : j + 1],
+                in0=position[:].unsqueeze(2),
+                scalar1=turns_coarse,
+                scalar2=None,
+                op0=ALU.mult,
+            )
+            nc.scalar.mul(
+                out=fine[:, :, j : j + 1], in_=position[:].unsqueeze(2), mul=turns - turns_coarse
+            )
+        whole = const.tile([P, TILES, PAIRS], F32)
+        nc.vector.tensor_scalar(
+            out=whole[:], in0=coarse[:], scalar1=ROUND, scalar2=ROUND, op0=ALU.add, op1=ALU.subtract
+        )
+        part = const.tile([P, TILES, PAIRS], F32)
+        nc.vector.tensor_tensor(out=part[:], in0=coarse[:], in1=whole[:], op=ALU.subtract)
+        both = const.tile([P, TILES, PAIRS], F32)
+        nc.vector.tensor_tensor(out=both[:], in0=part[:], in1=fine[:], op=ALU.add)
+        whole2 = const.tile([P, TILES, PAIRS], F32)
+        nc.vector.tensor_scalar(
+            out=whole2[:], in0=both[:], scalar1=ROUND, scalar2=ROUND, op0=ALU.add, op1=ALU.subtract
+        )
+        turn = const.tile([P, TILES, PAIRS], F32)
+        nc.vector.tensor_tensor(out=turn[:], in0=both[:], in1=whole2[:], op=ALU.subtract)
+        size = const.tile([P, TILES, PAIRS], F32)
+        nc.vector.scalar_tensor_tensor(
+            out=size[:], in0=turn[:], scalar=-1.0, in1=turn[:], op0=ALU.mult, op1=ALU.max
+        )
+        quarter = const.tile([P, TILES, PAIRS], F32)
+        nc.vector.tensor_scalar(
+            out=quarter[:], in0=size[:], scalar1=-1.0, scalar2=0.25, op0=ALU.mult, op1=ALU.add
+        )
+        cos_t = const.tile([P, TILES, HEADS, PAIRS], F32)
+        sin_t = const.tile([P, TILES, HEADS, PAIRS], F32)
+        nsin_t = const.tile([P, TILES, HEADS, PAIRS], F32)
+
+        def fill_tables(g):
+            tiles = slice(g * GROUP, (g + 1) * GROUP)
+            shape = [P, GROUP, HEADS, PAIRS]
+            for table, turns_of, scale in (
+                (cos_t, quarter, 2.0 * math.pi),
+                (sin_t, turn, 2.0 * math.pi),
+                (nsin_t, turn, -2.0 * math.pi),
+            ):
+                nc.scalar.activation(
+                    out=table[:, tiles],
+                    in_=turns_of[:, tiles].unsqueeze(2).to_broadcast(shape),
+                    func=ACT.Sin,
+                    scale=scale,
+                )
+
+        w_grouped = const.tile([P, FEATURES, 4], BF16, align_bytes=64)
+        by_head = w_raw[:].rearrange("p t (h d) -> p h d t", h=HEADS)
+        nc.vector.tensor_copy(
+            out=w_grouped[:, 0 : HEADS * NOPE_DIM, :].rearrange("p (h d) t -> p h d t", h=HEADS),
+            in_=by_head[:, :, 0:NOPE_DIM, :],
+        )
+        by_pair = by_head[:, :, NOPE_DIM:HEAD_DIM, :].rearrange("p h (j e) t -> p e h j t", e=2)
+        for e in range(2):
+            first = HEADS * (NOPE_DIM + e * PAIRS)
+            nc.vector.tensor_copy(
+                out=w_grouped[:, first : first + HEADS * PAIRS, :].rearrange(
+                    "p (h j) t -> p h j t", h=HEADS
+                ),
+                in_=by_pair[:, e],
+            )
+        w_codes = const.tile([P, FEATURES], U32, align_bytes=64)
+        w_scales = const.tile([P, FEATURES], U8, align_bytes=64)
+        nc.vector.quantize_mx(
+            out=w_codes[:].bitcast(FP8X4),
+            scales=w_scales[:],
+            in_=w_grouped[:].rearrange("p n t -> p (n t)"),
+        )
+
+        xt_of, grouped_of, codes_of, scales_of, y_of, stage_of, products_of = {}, {}, {}, {}, {}, {}, {}
+
+        def transpose_group(g):
+            x_words = x_of[g // GROUPS_PER_LOAD][:].bitcast(F32)
+            first = (g % GROUPS_PER_LOAD) * GROUP * WORDS
+            banks = []
+            for half in range(2):
+                xt = tpsum.tile([P, 2, 2, P], F32)
+                for i in range(2):
+                    for u in range(2):
+                        start = first + ((2 * half + i) * 2 + u) * P
+                        nc.tensor.transpose(xt[:, i, u, :], x_words[:, start : start + P], ident[:])
+                banks.append(xt)
+            xt_of[g] = banks
+
+        def regroup_group(g):
+            grouped = gpool.tile([P, GROUP * HID], BF16, align_bytes=64)
+            grouped_words = grouped[:].bitcast(F32).rearrange(
+                "p (half i r u) -> p half i r u", half=2, i=2, u=2
+            )
+            for half in range(2):
+                nc.scalar.copy(
+                    out=grouped_words[:, half],
+                    in_=xt_of[g][half][:].rearrange("p i u r -> p i r u"),
+                )
+            grouped_of[g] = grouped
+
+        def quantise_group(g):
+            codes = qpool.tile([P, GROUP * P], U32, align_bytes=64)
+            scales = qpool.tile([P, GROUP * P], U8, align_bytes=64)
+            nc.vector.quantize_mx(
+                out=codes[:].bitcast(FP8X4), scales=scales[:], in_=grouped_of[g][:]
+            )
+            codes_of[g] = codes
+            scales_of[g] = scales
+
+        def multiply_group(g):
+            y = ypsum.tile([P, GROUP, FEATURES], F32)
+            for i in range(GROUP):
+                tokens = slice(i * P, (i + 1) * P)
+                nc.tensor.matmul_mx(
+                    out=y[:, i, :],
+                    lhsT=codes_of[g][:, tokens].bitcast(FP8X4),
+                    lhsT_scale=scales_of[g][:, tokens],
+                    rhs=w_codes[:].bitcast(FP8X4),
+                    rhs_scale=w_scales[:],
+                    start=True,
+                    stop=True,
+                )
+            y_of[g] = y
+
+        def stage_part(g, features):
+            first = (g % GROUPS_PER_STORE) * GROUP
+            return stage_of[g // GROUPS_PER_STORE][:, :, first : first + GROUP, features]
+
+        def copy_unrotated(g):
+            if g % GROUPS_PER_STORE == 0:
+                stage = spool.tile([P, HEADS, STORE_TILES, HEAD_DIM], F32)
+                stage_of[g // GROUPS_PER_STORE] = stage
+            nc.scalar.copy(
+                out=stage_part(g, slice(0, NOPE_DIM)).rearrange("p h c d -> p c h d"),
+                in_=y_of[g][:, :, 0 : HEADS * NOPE_DIM].rearrange("p c (h d) -> p c h d", h=HEADS),
+            )
+
+        def rotate_products(g):
+            tiles = slice((g % GROUPS_PER_BATCH) * GROUP, (g % GROUPS_PER_BATCH + 1) * GROUP)
+            pair_halves = y_of[g][:, :, HEADS * NOPE_DIM : FEATURES].rearrange(
+                "p c (e x) -> p e c x", e=2
+            )
+            by_cos = rpool.tile([P, 2, ROTATED], F32)
+            by_sin = rpool.tile([P, 2, ROTATED], F32)
+            nc.vector.tensor_tensor(
+                out=by_cos[:].rearrange("p e (c x) -> p e c x", c=GROUP),
+                in0=pair_halves,
+                in1=cos_t[:, tiles]
+                .rearrange("p c h j -> p c (h j)")
+                .unsqueeze(1)
+                .to_broadcast([P, 2, GROUP, HEADS * PAIRS]),
+                op=ALU.mult,
+            )
+            for e, table in ((0, nsin_t), (1, sin_t)):
+                nc.vector.tensor_tensor(
+                    out=by_sin[:, e, :].rearrange("p (c x) -> p c x", c=GROUP),
+                    in0=pair_halves[:, 1 - e],
+                    in1=table[:, tiles].rearrange("p c h j -> p c (h j)"),
+                    op=ALU.mult,
+                )
+            products_of[g] = (by_cos, by_sin)
+
+        def rotate_sum(g):
+            by_cos, by_sin = products_of[g]
+            order = "p e (c h j) -> p c h j e"
+            nc.vector.tensor_tensor(
+                out=stage_part(g, slice(NOPE_DIM, HEAD_DIM)).rearrange(
+                    "p h c (j e) -> p c h j e", e=2
+                ),
+                in0=by_cos[:].rearrange(order, c=GROUP, h=HEADS),
+                in1=by_sin[:].rearrange(order, c=GROUP, h=HEADS),
+                op=ALU.add,
+            )
+
+        def store_group(g):
+            if g % GROUPS_PER_STORE == GROUPS_PER_STORE - 1:
+                b, first = divmod((g + 1) * GROUP - STORE_TILES, TILES)
+                nc.gpsimd.dma_start(
+                    out=out[b].rearrange("h (p c) d -> p h c d", c=TILES)[
+                        :, :, first : first + STORE_TILES, :
+                    ],
+                    in_=stage_of[g // GROUPS_PER_STORE][:],
+                )
+
+        for step in range(N_GROUPS + 3):
+            if step < N_GROUPS:
+                transpose_group(step)
+                regroup_group(step)
+            if step < GROUPS_PER_BATCH:
+                fill_tables(step)
+            if step >= 3:
+                rotate_products(step - 3)
+            if 1 <= step <= N_GROUPS:
+                quantise_group(step - 1)
+            if 2 <= step <= N_GROUPS + 1:
+                multiply_group(step - 2)
+                copy_unrotated(step - 2)
+            if step >= 3:
+                rotate_sum(step - 3)
+                store_group(step - 3)

@@ -30,6 +30,7 @@ STORE_TILES = 8
 N_GROUPS = BATCH * TILES // GROUP
 N_LOADS = BATCH * TILES // LOAD_TILES
 GROUPS_PER_LOAD = LOAD_TILES // GROUP
+LOADS_AHEAD = 12
 GROUPS_PER_STORE = STORE_TILES // GROUP
 GROUPS_PER_BATCH = TILES // GROUP
 ROTATED = GROUP * HEADS * PAIRS
@@ -42,7 +43,7 @@ def tile_deepseekv4attention_pb_t_kernel(tc, hidden, wq, out):
     nc = tc.nc
     with ExitStack() as ctx:
         const = ctx.enter_context(tc.tile_pool(name="const", bufs=1))
-        xpool = ctx.enter_context(tc.tile_pool(name="xpool", bufs=N_LOADS))
+        xpool = ctx.enter_context(tc.tile_pool(name="xpool", bufs=LOADS_AHEAD))
         gpool = ctx.enter_context(tc.tile_pool(name="gpool", bufs=3))
         qpool = ctx.enter_context(tc.tile_pool(name="qpool", bufs=3))
         rpool = ctx.enter_context(tc.tile_pool(name="rpool", bufs=2))
@@ -58,7 +59,8 @@ def tile_deepseekv4attention_pb_t_kernel(tc, hidden, wq, out):
                 in_=wq[WORDS * u : WORDS * (u + 1), :].rearrange("(q e) n -> q e n", e=2),
             )
         x_of = {}
-        for load in range(N_LOADS):
+
+        def load_tiles(load):
             b, first = divmod(load * LOAD_TILES, TILES)
             x_sb = xpool.tile([P, LOAD_TILES * HID], BF16)
             nc.sync.dma_start(
@@ -68,6 +70,9 @@ def tile_deepseekv4attention_pb_t_kernel(tc, hidden, wq, out):
                 ],
             )
             x_of[load] = x_sb
+
+        for load in range(LOADS_AHEAD):
+            load_tiles(load)
 
         position_i = const.tile([P, TILES], I32)
         nc.gpsimd.iota(position_i[:], pattern=[[1, TILES]], base=0, channel_multiplier=TILES)
@@ -264,7 +269,7 @@ def tile_deepseekv4attention_pb_t_kernel(tc, hidden, wq, out):
         def store_group(g):
             if g % GROUPS_PER_STORE == GROUPS_PER_STORE - 1:
                 b, first = divmod((g + 1) * GROUP - STORE_TILES, TILES)
-                nc.gpsimd.dma_start(
+                nc.sync.dma_start(
                     out=out[b].rearrange("h (p c) d -> p h c d", c=TILES)[
                         :, :, first : first + STORE_TILES, :
                     ],
@@ -275,6 +280,8 @@ def tile_deepseekv4attention_pb_t_kernel(tc, hidden, wq, out):
             if step < N_GROUPS:
                 transpose_group(step)
                 regroup_group(step)
+            if step + LOADS_AHEAD < N_LOADS:
+                load_tiles(step + LOADS_AHEAD)
             if step < GROUPS_PER_BATCH:
                 fill_tables(step)
             if step >= 3:

@@ -46,7 +46,7 @@ def tile_deepseekv4attention_pb_t_kernel(tc, hidden, wq, out):
         xpool = ctx.enter_context(tc.tile_pool(name="xpool", bufs=LOADS_AHEAD))
         gpool = ctx.enter_context(tc.tile_pool(name="gpool", bufs=3))
         qpool = ctx.enter_context(tc.tile_pool(name="qpool", bufs=3))
-        rpool = ctx.enter_context(tc.tile_pool(name="rpool", bufs=2))
+        rpool = ctx.enter_context(tc.tile_pool(name="rpool", bufs=3))
         spool = ctx.enter_context(tc.tile_pool(name="spool", bufs=6))
         tpsum = ctx.enter_context(tc.psum_pool(name="tpsum", bufs=4))
         ypsum = ctx.enter_context(tc.psum_pool(name="ypsum", bufs=4))
@@ -257,7 +257,7 @@ def tile_deepseekv4attention_pb_t_kernel(tc, hidden, wq, out):
         def rotate_sum(g):
             by_cos, by_sin = products_of[g]
             order = "p e (c h j) -> p c h j e"
-            nc.vector.tensor_tensor(
+            nc.gpsimd.tensor_tensor(
                 out=stage_part(g, slice(NOPE_DIM, HEAD_DIM)).rearrange(
                     "p h c (j e) -> p c h j e", e=2
                 ),

@@ -30,7 +30,7 @@ STORE_TILES = 8
 N_GROUPS = BATCH * TILES // GROUP
 N_LOADS = BATCH * TILES // LOAD_TILES
 GROUPS_PER_LOAD = LOAD_TILES // GROUP
-LOADS_AHEAD = 12
+LOADS_AHEAD = 32
 GROUPS_PER_STORE = STORE_TILES // GROUP
 GROUPS_PER_BATCH = TILES // GROUP
 ROTATED = GROUP * HEADS * PAIRS
@@ -46,8 +46,8 @@ def tile_deepseekv4attention_pb_t_kernel(tc, hidden, wq, out):
         xpool = ctx.enter_context(tc.tile_pool(name="xpool", bufs=LOADS_AHEAD))
         gpool = ctx.enter_context(tc.tile_pool(name="gpool", bufs=3))
         qpool = ctx.enter_context(tc.tile_pool(name="qpool", bufs=3))
-        rpool = ctx.enter_context(tc.tile_pool(name="rpool", bufs=3))
-        spool = ctx.enter_context(tc.tile_pool(name="spool", bufs=6))
+        rpool = ctx.enter_context(tc.tile_pool(name="rpool", bufs=2))
+        spool = ctx.enter_context(tc.tile_pool(name="spool", bufs=12))
         tpsum = ctx.enter_context(tc.psum_pool(name="tpsum", bufs=4))
         ypsum = ctx.enter_context(tc.psum_pool(name="ypsum", bufs=4))
         ctx.enter_context(tc.manual_schedule())
@@ -257,7 +257,7 @@ def tile_deepseekv4attention_pb_t_kernel(tc, hidden, wq, out):
         def rotate_sum(g):
             by_cos, by_sin = products_of[g]
             order = "p e (c h j) -> p c h j e"
-            nc.gpsimd.tensor_tensor(
+            nc.vector.tensor_tensor(
                 out=stage_part(g, slice(NOPE_DIM, HEAD_DIM)).rearrange(
                     "p h c (j e) -> p c h j e", e=2
                 ),

import math
from contextlib import ExitStack

import concourse.mybir as mybir
from concourse.masks import make_identity

F32 = mybir.dt.float32
BF16 = mybir.dt.bfloat16
I32 = mybir.dt.int32
U32 = mybir.dt.uint32
U8 = mybir.dt.uint8
FP8X4 = mybir.dt.float8_e4m3fn_x4
ALU = mybir.AluOpType
ACT = mybir.ActivationFunctionType

P = 128
BATCH, SEQ, HID = 4, 4096, 512
HEADS, HEAD_DIM, ROPE_DIM = 2, 64, 32
NOPE_DIM = HEAD_DIM - ROPE_DIM
PAIRS = ROPE_DIM // 2
FEATURES = HEADS * HEAD_DIM
THETA = 10000.0
FLOPS = 2 * BATCH * SEQ * HID * FEATURES

WORDS = HID // 2
TILES = SEQ // P
GROUP = 4
LOAD_TILES = 4
STORE_TILES = 8
N_GROUPS = BATCH * TILES // GROUP
N_LOADS = BATCH * TILES // LOAD_TILES
GROUPS_PER_LOAD = LOAD_TILES // GROUP
LOADS_AHEAD = 32
GROUPS_PER_STORE = STORE_TILES // GROUP
GROUPS_PER_BATCH = TILES // GROUP
ROTATED = GROUP * HEADS * PAIRS

ROUND = 1.5 * 2.0**23
COARSE = 2.0**14


def tile_deepseekv4attention_pb_t_kernel(tc, hidden, wq, out):
    nc = tc.nc
    with ExitStack() as ctx:
        const = ctx.enter_context(tc.tile_pool(name="const", bufs=1))
        xpool = ctx.enter_context(tc.tile_pool(name="xpool", bufs=LOADS_AHEAD))
        gpool = ctx.enter_context(tc.tile_pool(name="gpool", bufs=3))
        qpool = ctx.enter_context(tc.tile_pool(name="qpool", bufs=3))
        rpool = ctx.enter_context(tc.tile_pool(name="rpool", bufs=2))
        spool = ctx.enter_context(tc.tile_pool(name="spool", bufs=12))
        tpsum = ctx.enter_context(tc.psum_pool(name="tpsum", bufs=4))
        ypsum = ctx.enter_context(tc.psum_pool(name="ypsum", bufs=4))
        ctx.enter_context(tc.manual_schedule())

        w_raw = const.tile([P, 4, FEATURES], BF16)
        for u in range(2):
            nc.scalar.dma_start(
                out=w_raw[:, 2 * u : 2 * u + 2, :],
                in_=wq[WORDS * u : WORDS * (u + 1), :].rearrange("(q e) n -> q e n", e=2),
            )
        x_of = {}

        def load_tiles(load):
            b, first = divmod(load * LOAD_TILES, TILES)
            x_sb = xpool.tile([P, LOAD_TILES * HID], BF16)
            nc.sync.dma_start(
                out=x_sb[:],
                in_=hidden[b].rearrange("(p c) k -> p (c k)", c=TILES)[
                    :, first * HID : (first + LOAD_TILES) * HID
                ],
            )
            x_of[load] = x_sb

        for load in range(LOADS_AHEAD):
            load_tiles(load)

        position_i = const.tile([P, TILES], I32)
        nc.gpsimd.iota(position_i[:], pattern=[[1, TILES]], base=0, channel_multiplier=TILES)
        ident = const.tile([P, P], F32)
        make_identity(nc, ident[:])

        zero = const.tile([P, 1], F32)
        nc.vector.memset(zero[:], 0.0)
        warm = const.tile([P, 1], F32)
        nc.scalar.activation(out=warm[:], in_=zero[:], func=ACT.Sin)

        position = const.tile([P, TILES], F32)
        nc.vector.tensor_copy(out=position[:], in_=position_i[:])
        coarse = const.tile([P, TILES, PAIRS], F32)
        fine = const.tile([P, TILES, PAIRS], F32)
        for j in range(PAIRS):
            turns = THETA ** (-j / PAIRS) / (2.0 * math.pi)
            turns_coarse = round(turns * COARSE) / COARSE
            nc.vector.tensor_scalar(
                out=coarse[:, :, j : j + 1],
                in0=position[:].unsqueeze(2),
                scalar1=turns_coarse,
                scalar2=None,
                op0=ALU.mult,
            )
            nc.scalar.mul(
                out=fine[:, :, j : j + 1], in_=position[:].unsqueeze(2), mul=turns - turns_coarse
            )
        whole = const.tile([P, TILES, PAIRS], F32)
        nc.vector.tensor_scalar(
            out=whole[:], in0=coarse[:], scalar1=ROUND, scalar2=ROUND, op0=ALU.add, op1=ALU.subtract
        )
        part = const.tile([P, TILES, PAIRS], F32)
        nc.vector.tensor_tensor(out=part[:], in0=coarse[:], in1=whole[:], op=ALU.subtract)
        both = const.tile([P, TILES, PAIRS], F32)
        nc.vector.tensor_tensor(out=both[:], in0=part[:], in1=fine[:], op=ALU.add)
        whole2 = const.tile([P, TILES, PAIRS], F32)
        nc.vector.tensor_scalar(
            out=whole2[:], in0=both[:], scalar1=ROUND, scalar2=ROUND, op0=ALU.add, op1=ALU.subtract
        )
        turn = const.tile([P, TILES, PAIRS], F32)
        nc.vector.tensor_tensor(out=turn[:], in0=both[:], in1=whole2[:], op=ALU.subtract)
        size = const.tile([P, TILES, PAIRS], F32)
        nc.vector.scalar_tensor_tensor(
            out=size[:], in0=turn[:], scalar=-1.0, in1=turn[:], op0=ALU.mult, op1=ALU.max
        )
        quarter = const.tile([P, TILES, PAIRS], F32)
        nc.vector.tensor_scalar(
            out=quarter[:], in0=size[:], scalar1=-1.0, scalar2=0.25, op0=ALU.mult, op1=ALU.add
        )
        cos_t = const.tile([P, TILES, HEADS, PAIRS], F32)
        sin_t = const.tile([P, TILES, HEADS, PAIRS], F32)
        nsin_t = const.tile([P, TILES, HEADS, PAIRS], F32)

        def fill_tables(g):
            tiles = slice(g * GROUP, (g + 1) * GROUP)
            shape = [P, GROUP, HEADS, PAIRS]
            for table, turns_of, scale in (
                (cos_t, quarter, 2.0 * math.pi),
                (sin_t, turn, 2.0 * math.pi),
                (nsin_t, turn, -2.0 * math.pi),
            ):
                nc.scalar.activation(
                    out=table[:, tiles],
                    in_=turns_of[:, tiles].unsqueeze(2).to_broadcast(shape),
                    func=ACT.Sin,
                    scale=scale,
                )

        w_grouped = const.tile([P, FEATURES, 4], BF16, align_bytes=64)
        by_head = w_raw[:].rearrange("p t (h d) -> p h d t", h=HEADS)
        nc.vector.tensor_copy(
            out=w_grouped[:, 0 : HEADS * NOPE_DIM, :].rearrange("p (h d) t -> p h d t", h=HEADS),
            in_=by_head[:, :, 0:NOPE_DIM, :],
        )
        by_pair = by_head[:, :, NOPE_DIM:HEAD_DIM, :].rearrange("p h (j e) t -> p e h j t", e=2)
        for e in range(2):
            first = HEADS * (NOPE_DIM + e * PAIRS)
            nc.vector.tensor_copy(
                out=w_grouped[:, first : first + HEADS * PAIRS, :].rearrange(
                    "p (h j) t -> p h j t", h=HEADS
                ),
                in_=by_pair[:, e],
            )
        w_codes = const.tile([P, FEATURES], U32, align_bytes=64)
        w_scales = const.tile([P, FEATURES], U8, align_bytes=64)
        nc.vector.quantize_mx(
            out=w_codes[:].bitcast(FP8X4),
            scales=w_scales[:],
            in_=w_grouped[:].rearrange("p n t -> p (n t)"),
        )

        xt_of, grouped_of, codes_of, scales_of, y_of, stage_of, products_of = {}, {}, {}, {}, {}, {}, {}

        def transpose_group(g):
            x_words = x_of[g // GROUPS_PER_LOAD][:].bitcast(F32)
            first = (g % GROUPS_PER_LOAD) * GROUP * WORDS
            banks = []
            for half in range(2):
                xt = tpsum.tile([P, 2, 2, P], F32)
                for i in range(2):
                    for u in range(2):
                        start = first + ((2 * half + i) * 2 + u) * P
                        nc.tensor.transpose(xt[:, i, u, :], x_words[:, start : start + P], ident[:])
                banks.append(xt)
            xt_of[g] = banks

        def regroup_group(g):
            grouped = gpool.tile([P, GROUP * HID], BF16, align_bytes=64)
            grouped_words = grouped[:].bitcast(F32).rearrange(
                "p (half i r u) -> p half i r u", half=2, i=2, u=2
            )
            for half in range(2):
                nc.scalar.copy(
                    out=grouped_words[:, half],
                    in_=xt_of[g][half][:].rearrange("p i u r -> p i r u"),
                )
            grouped_of[g] = grouped

        def quantise_group(g):
            codes = qpool.tile([P, GROUP * P], U32, align_bytes=64)
            scales = qpool.tile([P, GROUP * P], U8, align_bytes=64)
            nc.vector.quantize_mx(
                out=codes[:].bitcast(FP8X4), scales=scales[:], in_=grouped_of[g][:]
            )
            codes_of[g] = codes
            scales_of[g] = scales

        def multiply_group(g):
            y = ypsum.tile([P, GROUP, FEATURES], F32)
            for i in range(GROUP):
                tokens = slice(i * P, (i + 1) * P)
                nc.tensor.matmul_mx(
                    out=y[:, i, :],
                    lhsT=codes_of[g][:, tokens].bitcast(FP8X4),
                    lhsT_scale=scales_of[g][:, tokens],
                    rhs=w_codes[:].bitcast(FP8X4),
                    rhs_scale=w_scales[:],
                    start=True,
                    stop=True,
                )
            y_of[g] = y

        def stage_part(g, features):
            first = (g % GROUPS_PER_STORE) * GROUP
            return stage_of[g // GROUPS_PER_STORE][:, :, first : first + GROUP, features]

        def copy_unrotated(g):
            if g % GROUPS_PER_STORE == 0:
                stage = spool.tile([P, HEADS, STORE_TILES, HEAD_DIM], F32)
                stage_of[g // GROUPS_PER_STORE] = stage
            nc.scalar.copy(
                out=stage_part(g, slice(0, NOPE_DIM)).rearrange("p h c d -> p c h d"),
                in_=y_of[g][:, :, 0 : HEADS * NOPE_DIM].rearrange("p c (h d) -> p c h d", h=HEADS),
            )

        def rotate_products(g):
            tiles = slice((g % GROUPS_PER_BATCH) * GROUP, (g % GROUPS_PER_BATCH + 1) * GROUP)
            pair_halves = y_of[g][:, :, HEADS * NOPE_DIM : FEATURES].rearrange(
                "p c (e x) -> p e c x", e=2
            )
            by_cos = rpool.tile([P, 2, ROTATED], F32)
            by_sin = rpool.tile([P, 2, ROTATED], F32)
            nc.vector.tensor_tensor(
                out=by_cos[:].rearrange("p e (c x) -> p e c x", c=GROUP),
                in0=pair_halves,
                in1=cos_t[:, tiles]
                .rearrange("p c h j -> p c (h j)")
                .unsqueeze(1)
                .to_broadcast([P, 2, GROUP, HEADS * PAIRS]),
                op=ALU.mult,
            )
            for e, table in ((0, nsin_t), (1, sin_t)):
                nc.vector.tensor_tensor(
                    out=by_sin[:, e, :].rearrange("p (c x) -> p c x", c=GROUP),
                    in0=pair_halves[:, 1 - e],
                    in1=table[:, tiles].rearrange("p c h j -> p c (h j)"),
                    op=ALU.mult,
                )
            products_of[g] = (by_cos, by_sin)

        def rotate_sum(g):
            by_cos, by_sin = products_of[g]
            order = "p e (c h j) -> p c h j e"
            nc.vector.tensor_tensor(
                out=stage_part(g, slice(NOPE_DIM, HEAD_DIM)).rearrange(
                    "p h c (j e) -> p c h j e", e=2
                ),
                in0=by_cos[:].rearrange(order, c=GROUP, h=HEADS),
                in1=by_sin[:].rearrange(order, c=GROUP, h=HEADS),
                op=ALU.add,
            )

        def store_group(g):
            if g % GROUPS_PER_STORE == GROUPS_PER_STORE - 1:
                b, first = divmod((g + 1) * GROUP - STORE_TILES, TILES)
                nc.sync.dma_start(
                    out=out[b].rearrange("h (p c) d -> p h c d", c=TILES)[
                        :, :, first : first + STORE_TILES, :
                    ],
                    in_=stage_of[g // GROUPS_PER_STORE][:],
                )

        for step in range(N_GROUPS + 3):
            if step < N_GROUPS:
                transpose_group(step)
                regroup_group(step)
            if step + LOADS_AHEAD < N_LOADS:
                load_tiles(step + LOADS_AHEAD)
            if step < GROUPS_PER_BATCH:
                fill_tables(step)
            if step >= 3:
                rotate_products(step - 3)
            if 1 <= step <= N_GROUPS:
                quantise_group(step - 1)
            if 2 <= step <= N_GROUPS + 1:
                multiply_group(step - 2)
                copy_unrotated(step - 2)
            if step >= 3:
                rotate_sum(step - 3)
                store_group(step - 3)
